import numpy as np
import ml_dtypes


def mxq(x, axis, fmt="e4m3"):
    dtype, down = {"e4m3": (ml_dtypes.float8_e4m3fn, 7), "e5m2": (ml_dtypes.float8_e5m2, 14)}[fmt]
    v = np.moveaxis(np.asarray(x, np.float32).astype(ml_dtypes.bfloat16).astype(np.float64), axis, -1)
    blocks = v.reshape(v.shape[:-1] + (-1, 32))
    amax = np.abs(blocks).max(-1, keepdims=True)
    byte = np.maximum(np.where(amax > 0, np.frexp(amax)[1] - 1 + 127, 0) - down, 1)
    scale = np.exp2(byte - 127.0)
    codes = (blocks / scale).astype(np.float32).astype(dtype).astype(np.float64)
    return np.moveaxis((codes * scale).reshape(v.shape), -1, axis)


WIDE = False


def mx_kscale(k):
    if not WIDE:
        return np.ones(k)
    levels = np.array([10, -10, 5, -5, 0])
    if k % 512:
        return np.exp2(np.random.permutation(np.resize(levels, k // 32))).repeat(32)
    a = np.empty((k // 512, 16))
    for p in range(k // 512):
        a[p, :8] = np.random.permutation(np.resize(levels, 8))
        for g in range(8):
            far = levels[np.abs(levels - a[p, g]) >= 10]
            a[p, g + 8] = far[np.random.randint(len(far))]
    return np.exp2(a.ravel()).repeat(32)


BF16 = ml_dtypes.bfloat16


def bf(x):
    return np.asarray(x, np.float32).astype(BF16)


def f64(x):
    return np.asarray(x).astype(np.float64)


N, M, K = 6, 512, 128
DIM = 1
DROP_P = 0.1


def setup_inputs():
    s = mx_kscale(M)
    r = s / s.max()
    x1 = np.random.standard_normal((1, N, M, K)) * np.sqrt(2.5) / K ** 0.25 * r[None, None, :, None]
    u = np.random.random((N, N, M, M))
    dropout_mask = (u >= DROP_P).astype(np.float64) / (1.0 - DROP_P) / r[None, None, None, :]
    return {"x1": bf(x1), "dropout_mask": bf(dropout_mask)}


def reference(x1, dropout_mask):
    x = f64(x1)
    scale = np.sqrt(DIM)
    key_t = x.transpose(1, 0, 2, 3)
    qk = x @ key_t.swapaxes(-2, -1)
    z = qk * scale
    e = np.exp(z - z.max(-1, keepdims=True))
    attn = e / e.sum(-1, keepdims=True)
    dropped = attn * f64(dropout_mask)
    return mxq(dropped, 3, "e4m3") @ mxq(x, 2, "e4m3")

@@ -1,0 +1,335 @@
+from contextlib import ExitStack
+
+import concourse.mybir as mybir
+from concourse.masks import make_identity
+
+F32 = mybir.dt.float32
+BF16 = mybir.dt.bfloat16
+U32 = mybir.dt.uint32
+U8 = mybir.dt.uint8
+FP8X4 = mybir.dt.float8_e4m3fn_x4
+ACT = mybir.ActivationFunctionType
+ALU = mybir.AluOpType
+AX = mybir.AxisListType
+
+NG = 6
+ROWS = 512
+D = 128
+P = 128
+MT = 4
+FLOPS = 2 * 2 * NG * NG * ROWS * ROWS * D
+
+PF = 8
+
+
+def tile_model_kernel(tc, x1, dropout_mask, out):
+    nc = tc.nc
+    pairs = [(i, j) for i in range(NG) for j in range(NG)]
+    npairs = len(pairs)
+    with ExitStack() as ctx:
+        const = ctx.enter_context(tc.tile_pool(name="const", bufs=1))
+        mpool = ctx.enter_context(tc.tile_pool(name="mask", bufs=PF))
+        epool = ctx.enter_context(tc.tile_pool(name="expo", bufs=12))
+        dpool = ctx.enter_context(tc.tile_pool(name="drop", bufs=6))
+        gpool = ctx.enter_context(tc.tile_pool(name="grouped", bufs=4))
+        qpool = ctx.enter_context(tc.tile_pool(name="quant", bufs=4))
+        opool = ctx.enter_context(tc.tile_pool(name="outs", bufs=4))
+        spool = ctx.enter_context(tc.tile_pool(name="stats", bufs=5))
+        gps = ctx.enter_context(tc.psum_pool(name="gps", bufs=4))
+        tps = ctx.enter_context(tc.psum_pool(name="tps", bufs=2))
+        ops = ctx.enter_context(tc.psum_pool(name="ops", bufs=1))
+
+        warm = const.tile([P, 1], F32, name="warm")
+        warm2 = const.tile([P, 1], F32, name="warm2")
+        nc.vector.memset(warm[:], 0.0)
+        nc.scalar.activation(out=warm2[:], in_=warm[:], func=ACT.Exp)
+
+        ident = const.tile([P, P], BF16, name="ident")
+        make_identity(nc, ident[:])
+
+        xc = const.tile([P, NG, MT, D], BF16, name="xc")
+        x4 = const.tile([P, NG, MT, D], BF16, name="x4")
+        xtm = const.tile([P, NG, MT, P], BF16, name="xtm")
+        xtn = const.tile([P, NG, MT, P], BF16, name="xtn")
+        xg = const.tile([P, NG, D, MT], BF16, name="xg", align_bytes=64)
+        xq = const.tile([P, NG * D], U32, name="xq", align_bytes=64)
+        xs = const.tile([P, NG * D], U8, name="xs", align_bytes=64)
+
+        mk = {}
+        nmax = {}
+        ssum = {}
+        rs = {}
+        gt = {}
+        et = {}
+        dd = {}
+        xt = {}
+        grp = {}
+        cod = {}
+        ot = {}
+        stp = {}
+        osb = {}
+
+        def load(q):
+            i, j = pairs[q]
+            m = mpool.tile([P, MT, ROWS], BF16, name="mk")
+            nc.sync.dma_start(
+                out=m[:], in_=dropout_mask[i, j].rearrange("(p t) n -> p t n", t=MT)
+            )
+            mk[q] = m
+
+        def setup_pe(j0, n):
+            st = tps.tile([P, 2, MT, P], BF16, name="xt")
+            for a in range(n):
+                for c in range(MT):
+                    nc.tensor.transpose(st[:, a, c, :], xc[:, j0 + a, c, :], ident[:])
+            stp[j0] = st
+
+        def setup_s(j0, n):
+            nc.scalar.copy(out=xtn[:, j0 : j0 + n], in_=stp[j0][:, 0:n])
+
+        def setup_v(j):
+            nc.vector.tensor_scalar_mul(
+                out=xtm[:, j],
+                in0=xtn[:, j].rearrange("k c p -> k (c p)").rearrange(
+                    "k (p t) -> k t p", t=MT
+                ),
+                scalar1=-1.0,
+            )
+
+        def setup_g(j):
+            nc.gpsimd.tensor_scalar(
+                out=xg[:, j],
+                in0=x4[:, j].rearrange("p c k -> p k c"),
+                scalar1=1.0,
+                scalar2=0.0,
+                op0=ALU.mult,
+                op1=ALU.add,
+            )
+
+        def qk(q):
+            i, j = pairs[q]
+            for t in range(MT):
+                g = gps.tile([P, ROWS], F32, tag="g", name="g")
+                nc.tensor.matmul(
+                    out=g[:],
+                    lhsT=xtm[:, j, t, :],
+                    rhs=xtn[:, i].rearrange("k c p -> k (c p)"),
+                    start=True,
+                    stop=True,
+                )
+                gt[(q, t)] = g
+
+        def vmin(q, t):
+            if t == 0:
+                nmax[q] = spool.tile([P, MT], F32, name="nmax")
+                ssum[q] = spool.tile([P, MT], F32, name="ssum")
+            nc.vector.tensor_reduce(
+                out=nmax[q][:, t : t + 1], in_=gt[(q, t)][:], axis=AX.X, op=ALU.min
+            )
+
+        def sexp(q, t):
+            e = epool.tile([P, ROWS], F32, name="e")
+            nc.scalar.activation(
+                out=e[:],
+                in_=gt[(q, t)][:],
+                func=ACT.Exp,
+                bias=nmax[q][:, t : t + 1],
+                scale=-1.0,
+                accum_out=ssum[q][:, t : t + 1],
+            )
+            et[(q, t)] = e
+
+        def recip(q):
+            rs[q] = spool.tile([P, MT], F32, name="rs")
+            nc.vector.reciprocal(out=rs[q][:], in_=ssum[q][:])
+
+        def vmul(q, t):
+            d = dpool.tile([P, ROWS], BF16, name="d")
+            nc.vector.scalar_tensor_tensor(
+                out=d[:],
+                in0=et[(q, t)][:],
+                scalar=rs[q][:, t : t + 1],
+                in1=mk[q][:, t, :],
+                op0=ALU.mult,
+                op1=ALU.mult,
+            )
+            dd[(q, t)] = d
+
+        def gmul(q, t):
+            d = dpool.tile([P, ROWS], BF16, name="d")
+            e = et[(q, t)]
+            nc.gpsimd.tensor_tensor(out=e[:], in0=e[:], in1=mk[q][:, t, :], op=ALU.mult)
+            nc.gpsimd.tensor_scalar(
+                out=d[:],
+                in0=e[:],
+                scalar1=rs[q][:, t : t + 1],
+                scalar2=0.0,
+                op0=ALU.mult,
+                op1=ALU.add,
+            )
+            dd[(q, t)] = d
+
+        def tr(q, t):
+            h, a = divmod(t, 2)
+            if a == 0:
+                xt[(q, h)] = tps.tile([P, 2, MT, P], BF16, name="xt")
+            for c in range(MT):
+                nc.tensor.transpose(
+                    xt[(q, h)][:, a, c, :], dd[(q, t)][:, c::MT], ident[:]
+                )
+
+        def cpy(q, h, eng):
+            if q not in grp:
+                grp[q] = gpool.tile([P, MT, P, MT], BF16, name="grp", align_bytes=64)
+            dst = grp[q][:, 2 * h : 2 * h + 2]
+            src = xt[(q, h)][:].rearrange("p a c m -> p a m c")
+            if eng == "v":
+                nc.vector.tensor_copy(out=dst, in_=src)
+            else:
+                nc.scalar.copy(out=dst, in_=src)
+
+        def quant_x(j):
+            nc.vector.quantize_mx(
+                out=xq[:, j * D : (j + 1) * D].bitcast(FP8X4),
+                scales=xs[:, j * D : (j + 1) * D],
+                in_=xg[:, j].rearrange("p k c -> p (k c)"),
+            )
+
+        def quant(q):
+            codes = qpool.tile([P, ROWS], U32, name="codes", align_bytes=64)
+            scl = qpool.tile([P, ROWS], U8, name="scl", align_bytes=64)
+            nc.vector.quantize_mx(
+                out=codes[:].bitcast(FP8X4),
+                scales=scl[:],
+                in_=grp[q][:].rearrange("p a m c -> p (a m c)"),
+            )
+            cod[q] = (codes, scl)
+
+        def mx(q, spare):
+            i, j = pairs[q]
+            if spare:
+                ot[q] = (
+                    gps.tile([P, 2, D], F32, tag="g", name="oga"),
+                    gps.tile([P, 2, D], F32, tag="g", name="ogb"),
+                )
+            else:
+                ot[q] = (
+                    ops.tile([P, 2, D], F32, name="oa"),
+                    ops.tile([P, 2, D], F32, name="ob2"),
+                )
+            codes, scl = cod[q]
+            for a in range(MT):
+                nc.tensor.matmul_mx(
+                    out=ot[q][a // 2][:, a % 2, :],
+                    lhsT=codes[:, a * P : (a + 1) * P].bitcast(FP8X4),
+                    lhsT_scale=scl[:, a * P : (a + 1) * P],
+                    rhs=xq[:, j * D : (j + 1) * D].bitcast(FP8X4),
+                    rhs_scale=xs[:, j * D : (j + 1) * D],
+                    start=True,
+                    stop=True,
+                )
+
+        def ocopy_v(q):
+            osb[q] = opool.tile([P, MT, D], F32, name="ob")
+            nc.vector.tensor_copy(out=osb[q][:, 0:2], in_=ot[q][0][:])
+
+        def ocopy_s(q):
+            i, j = pairs[q]
+            nc.scalar.copy(out=osb[q][:, 2:4], in_=ot[q][1][:])
+            nc.sync.dma_start(
+                out=out[i, j].rearrange("(p t) k -> p t k", t=MT), in_=osb[q][:]
+            )
+
+        nc.sync.dma_start(
+            out=xc[:, 0], in_=x1[0, 0].rearrange("(c p) k -> p c k", p=P)
+        )
+        nc.sync.dma_start(
+            out=xc[:, 1:], in_=x1[0, 1:].rearrange("j (c p) k -> p j c k", p=P)
+        )
+        load(0)
+        nc.sync.dma_start(
+            out=x4[:], in_=x1[0].rearrange("j (p c) k -> p j c k", c=MT)
+        )
+        for q in range(1, PF):
+            load(q)
+
+        ctx.enter_context(tc.manual_schedule())
+
+        setup_pe(0, 1)
+        setup_s(0, 1)
+        setup_v(0)
+        for j in range(NG):
+            setup_g(j)
+        qk(0)
+        setup_pe(1, 1)
+        vmin(0, 0)
+        sexp(0, 0)
+        setup_s(1, 1)
+        for t in range(1, MT):
+            vmin(0, t)
+            sexp(0, t)
+        setup_v(1)
+        qk(1)
+        setup_pe(2, 2)
+        setup_s(2, 2)
+        setup_pe(4, 2)
+
+        last = npairs - 1
+        for p in range(last):
+            if p > 0:
+                recip(p)
+                gmul(p, 3)
+            if p >= 3:
+                mx(p - 3, False)
+            if p >= 1:
+                cpy(p - 1, 0, "s")
+            for t in range(MT):
+                vmin(p + 1, t)
+                sexp(p + 1, t)
+            if p == 0:
+                recip(p)
+                setup_s(4, 2)
+            if p + 2 < NG:
+                setup_v(p + 2)
+            if p + 2 < npairs:
+                qk(p + 2)
+            if p >= 3:
+                ocopy_v(p - 3)
+            if p >= 1:
+                cpy(p - 1, 1, "s")
+            if p >= 3:
+                ocopy_s(p - 3)
+            for t in range(MT):
+                if t < 3 or p == 0:
+                    vmul(p, t)
+                tr(p, t)
+            if 0 <= p - 2 < NG:
+                quant_x(p - 2)
+            if p >= 2:
+                quant(p - 2)
+            if p + PF < npairs:
+                load(p + PF)
+
+        recip(last)
+        mx(last - 3, False)
+        cpy(last - 1, 0, "s")
+        for t in range(MT):
+            vmul(last, t)
+            tr(last, t)
+        cpy(last - 1, 1, "s")
+        quant(last - 2)
+        mx(last - 2, True)
+        ocopy_v(last - 3)
+        ocopy_s(last - 3)
+        cpy(last, 0, "s")
+        quant(last - 1)
+        mx(last - 1, True)
+        cpy(last, 1, "v")
+        ocopy_v(last - 2)
+        ocopy_s(last - 2)
+        quant(last)
+        mx(last, False)
+        ocopy_v(last - 1)
+        ocopy_s(last - 1)
+        ocopy_v(last)
+        ocopy_s(last)

@@ -37,7 +37,7 @@ def tile_model_kernel(tc, x1, dropout_mask, out):
         spool = ctx.enter_context(tc.tile_pool(name="stats", bufs=5))
         gps = ctx.enter_context(tc.psum_pool(name="gps", bufs=4))
         tps = ctx.enter_context(tc.psum_pool(name="tps", bufs=2))
-        ops = ctx.enter_context(tc.psum_pool(name="ops", bufs=1))
+        ops = ctx.enter_context(tc.psum_pool(name="ops", bufs=2))
 
         warm = const.tile([P, 1], F32, name="warm")
         warm2 = const.tile([P, 1], F32, name="warm2")
@@ -46,9 +46,10 @@ def tile_model_kernel(tc, x1, dropout_mask, out):
 
         ident = const.tile([P, P], BF16, name="ident")
         make_identity(nc, ident[:])
+        ident32 = const.tile([P, P], F32, name="ident32")
+        make_identity(nc, ident32[:])
 
         xc = const.tile([P, NG, MT, D], BF16, name="xc")
-        x4 = const.tile([P, NG, MT, D], BF16, name="x4")
         xtm = const.tile([P, NG, MT, P], BF16, name="xtm")
         xtn = const.tile([P, NG, MT, P], BF16, name="xtn")
         xg = const.tile([P, NG, D, MT], BF16, name="xg", align_bytes=64)
@@ -85,7 +86,12 @@ def tile_model_kernel(tc, x1, dropout_mask, out):
             stp[j0] = st
 
         def setup_s(j0, n):
-            nc.scalar.copy(out=xtn[:, j0 : j0 + n], in_=stp[j0][:, 0:n])
+            nc.scalar.copy(
+                out=xtn[:, j0 : j0 + n].rearrange("k a c p -> k a (c p)").rearrange(
+                    "k a (p t) -> k a p t", t=MT
+                ),
+                in_=stp[j0][:, 0:n].rearrange("k a c p -> k a p c"),
+            )
 
         def setup_v(j):
             nc.vector.tensor_scalar_mul(
@@ -99,7 +105,7 @@ def tile_model_kernel(tc, x1, dropout_mask, out):
         def setup_g(j):
             nc.gpsimd.tensor_scalar(
                 out=xg[:, j],
-                in0=x4[:, j].rearrange("p c k -> p k c"),
+                in0=xc[:, j].rearrange("p c k -> p k c"),
                 scalar1=1.0,
                 scalar2=0.0,
                 op0=ALU.mult,
@@ -172,17 +178,21 @@ def tile_model_kernel(tc, x1, dropout_mask, out):
         def tr(q, t):
             h, a = divmod(t, 2)
             if a == 0:
-                xt[(q, h)] = tps.tile([P, 2, MT, P], BF16, name="xt")
-            for c in range(MT):
-                nc.tensor.transpose(
-                    xt[(q, h)][:, a, c, :], dd[(q, t)][:, c::MT], ident[:]
-                )
+                xt[(q, h)] = tps.tile([P, 2, 2, P], F32, name="xt")
+            words = dd[(q, t)][:].bitcast(F32)
+            for u in range(2):
+                nc.tensor.transpose(xt[(q, h)][:, a, u, :], words[:, u::2], ident32[:])
 
         def cpy(q, h, eng):
             if q not in grp:
                 grp[q] = gpool.tile([P, MT, P, MT], BF16, name="grp", align_bytes=64)
-            dst = grp[q][:, 2 * h : 2 * h + 2]
-            src = xt[(q, h)][:].rearrange("p a c m -> p a m c")
+            dst = (
+                grp[q][:, 2 * h : 2 * h + 2]
+                .rearrange("p a m c -> p (a m c)")
+                .bitcast(F32)
+                .rearrange("p (a m u) -> p a m u", a=2, u=2)
+            )
+            src = xt[(q, h)][:].rearrange("p a u m -> p a m u")
             if eng == "v":
                 nc.vector.tensor_copy(out=dst, in_=src)
             else:
@@ -208,19 +218,13 @@ def tile_model_kernel(tc, x1, dropout_mask, out):
         def mx(q, spare):
             i, j = pairs[q]
             if spare:
-                ot[q] = (
-                    gps.tile([P, 2, D], F32, tag="g", name="oga"),
-                    gps.tile([P, 2, D], F32, tag="g", name="ogb"),
-                )
+                ot[q] = gps.tile([P, MT, D], F32, tag="g", name="og")
             else:
-                ot[q] = (
-                    ops.tile([P, 2, D], F32, name="oa"),
-                    ops.tile([P, 2, D], F32, name="ob2"),
-                )
+                ot[q] = ops.tile([P, MT, D], F32, name="oa")
             codes, scl = cod[q]
             for a in range(MT):
                 nc.tensor.matmul_mx(
-                    out=ot[q][a // 2][:, a % 2, :],
+                    out=ot[q][:, a, :],
                     lhsT=codes[:, a * P : (a + 1) * P].bitcast(FP8X4),
                     lhsT_scale=scl[:, a * P : (a + 1) * P],
                     rhs=xq[:, j * D : (j + 1) * D].bitcast(FP8X4),
@@ -229,28 +233,21 @@ def tile_model_kernel(tc, x1, dropout_mask, out):
                     stop=True,
                 )
 
-        def ocopy_v(q):
-            osb[q] = opool.tile([P, MT, D], F32, name="ob")
-            nc.vector.tensor_copy(out=osb[q][:, 0:2], in_=ot[q][0][:])
-
         def ocopy_s(q):
             i, j = pairs[q]
-            nc.scalar.copy(out=osb[q][:, 2:4], in_=ot[q][1][:])
+            osb[q] = opool.tile([P, MT, D], F32, name="ob")
+            nc.scalar.copy(out=osb[q][:], in_=ot[q][:])
             nc.sync.dma_start(
                 out=out[i, j].rearrange("(p t) k -> p t k", t=MT), in_=osb[q][:]
             )
 
         nc.sync.dma_start(
-            out=xc[:, 0], in_=x1[0, 0].rearrange("(c p) k -> p c k", p=P)
+            out=xc[:, 0], in_=x1[0, 0].rearrange("(p c) k -> p c k", c=MT)
         )
         nc.sync.dma_start(
-            out=xc[:, 1:], in_=x1[0, 1:].rearrange("j (c p) k -> p j c k", p=P)
+            out=xc[:, 1:], in_=x1[0, 1:].rearrange("j (p c) k -> p j c k", c=MT)
         )
-        load(0)
-        nc.sync.dma_start(
-            out=x4[:], in_=x1[0].rearrange("j (p c) k -> p j c k", c=MT)
-        )
-        for q in range(1, PF):
+        for q in range(PF):
             load(q)
 
         ctx.enter_context(tc.manual_schedule())
@@ -293,8 +290,6 @@ def tile_model_kernel(tc, x1, dropout_mask, out):
                 setup_v(p + 2)
             if p + 2 < npairs:
                 qk(p + 2)
-            if p >= 3:
-                ocopy_v(p - 3)
             if p >= 1:
                 cpy(p - 1, 1, "s")
             if p >= 3:
@@ -319,17 +314,13 @@ def tile_model_kernel(tc, x1, dropout_mask, out):
         cpy(last - 1, 1, "s")
         quant(last - 2)
         mx(last - 2, True)
-        ocopy_v(last - 3)
         ocopy_s(last - 3)
         cpy(last, 0, "s")
         quant(last - 1)
         mx(last - 1, True)
         cpy(last, 1, "v")
-        ocopy_v(last - 2)
         ocopy_s(last - 2)
         quant(last)
         mx(last, False)
-        ocopy_v(last - 1)
         ocopy_s(last - 1)
-        ocopy_v(last)
         ocopy_s(last)

@@ -164,15 +164,15 @@ def tile_model_kernel(tc, x1, dropout_mask, out):
         def gmul(q, t):
             d = dpool.tile([P, ROWS], BF16, name="d")
             e = et[(q, t)]
-            nc.gpsimd.tensor_tensor(out=e[:], in0=e[:], in1=mk[q][:, t, :], op=ALU.mult)
             nc.gpsimd.tensor_scalar(
-                out=d[:],
+                out=e[:],
                 in0=e[:],
                 scalar1=rs[q][:, t : t + 1],
                 scalar2=0.0,
                 op0=ALU.mult,
                 op1=ALU.add,
             )
+            nc.gpsimd.tensor_tensor(out=d[:], in0=e[:], in1=mk[q][:, t, :], op=ALU.mult)
             dd[(q, t)] = d
 
         def tr(q, t):
@@ -274,7 +274,6 @@ def tile_model_kernel(tc, x1, dropout_mask, out):
         last = npairs - 1
         for p in range(last):
             if p > 0:
-                recip(p)
                 gmul(p, 3)
             if p >= 3:
                 mx(p - 3, False)
@@ -300,12 +299,12 @@ def tile_model_kernel(tc, x1, dropout_mask, out):
                 tr(p, t)
             if 0 <= p - 2 < NG:
                 quant_x(p - 2)
+            recip(p + 1)
             if p >= 2:
                 quant(p - 2)
             if p + PF < npairs:
                 load(p + PF)
 
-        recip(last)
         mx(last - 3, False)
         cpy(last - 1, 0, "s")
         for t in range(MT):

@@ -24,8 +24,9 @@ PF = 8
 
 def tile_model_kernel(tc, x1, dropout_mask, out):
     nc = tc.nc
-    pairs = [(i, j) for i in range(NG) for j in range(NG)]
+    pairs = [(i, j) for j in range(NG) for i in range(NG)]
     npairs = len(pairs)
+    last = npairs - 1
     with ExitStack() as ctx:
         const = ctx.enter_context(tc.tile_pool(name="const", bufs=1))
         mpool = ctx.enter_context(tc.tile_pool(name="mask", bufs=PF))
@@ -51,7 +52,7 @@ def tile_model_kernel(tc, x1, dropout_mask, out):
 
         xc = const.tile([P, NG, MT, D], BF16, name="xc")
         xtm = const.tile([P, NG, MT, P], BF16, name="xtm")
-        xtn = const.tile([P, NG, MT, P], BF16, name="xtn")
+        xtn = const.tile([P, NG, ROWS], BF16, name="xtn")
         xg = const.tile([P, NG, D, MT], BF16, name="xg", align_bytes=64)
         xq = const.tile([P, NG * D], U32, name="xq", align_bytes=64)
         xs = const.tile([P, NG * D], U8, name="xs", align_bytes=64)
@@ -68,7 +69,6 @@ def tile_model_kernel(tc, x1, dropout_mask, out):
         cod = {}
         ot = {}
         stp = {}
-        osb = {}
 
         def load(q):
             i, j = pairs[q]
@@ -78,28 +78,29 @@ def tile_model_kernel(tc, x1, dropout_mask, out):
             )
             mk[q] = m
 
-        def setup_pe(j0, n):
-            st = tps.tile([P, 2, MT, P], BF16, name="xt")
-            for a in range(n):
-                for c in range(MT):
-                    nc.tensor.transpose(st[:, a, c, :], xc[:, j0 + a, c, :], ident[:])
-            stp[j0] = st
+        def setup_pe(g, pool):
+            if pool == "t":
+                st = tps.tile([P, MT, P], BF16, tag="xt", name="stt")
+            else:
+                st = ops.tile([P, MT, P], BF16, tag="oa", name="sto")
+            for c in range(MT):
+                nc.tensor.transpose(st[:, c, :], xc[:, g, c, :], ident[:])
+            stp[(g, pool)] = st
 
-        def setup_s(j0, n):
+        def setup_n(g):
             nc.scalar.copy(
-                out=xtn[:, j0 : j0 + n].rearrange("k a c p -> k a (c p)").rearrange(
-                    "k a (p t) -> k a p t", t=MT
-                ),
-                in_=stp[j0][:, 0:n].rearrange("k a c p -> k a p c"),
+                out=xtn[:, g].rearrange("k (p t) -> k p t", t=MT),
+                in_=stp[(g, "o")][:].rearrange("k t p -> k p t"),
             )
 
-        def setup_v(j):
-            nc.vector.tensor_scalar_mul(
-                out=xtm[:, j],
-                in0=xtn[:, j].rearrange("k c p -> k (c p)").rearrange(
-                    "k (p t) -> k t p", t=MT
-                ),
-                scalar1=-1.0,
+        def setup_m0():
+            nc.vector.tensor_scalar_mul(out=xtm[:, 0], in0=stp[(0, "t")][:], scalar1=-1.0)
+
+        def setup_m(g):
+            nc.scalar.mul(
+                out=xtm[:, g],
+                in_=xtn[:, g].rearrange("k (p t) -> k t p", t=MT),
+                mul=-1.0,
             )
 
         def setup_g(j):
@@ -117,11 +118,7 @@ def tile_model_kernel(tc, x1, dropout_mask, out):
             for t in range(MT):
                 g = gps.tile([P, ROWS], F32, tag="g", name="g")
                 nc.tensor.matmul(
-                    out=g[:],
-                    lhsT=xtm[:, j, t, :],
-                    rhs=xtn[:, i].rearrange("k c p -> k (c p)"),
-                    start=True,
-                    stop=True,
+                    out=g[:], lhsT=xtm[:, j, t, :], rhs=xtn[:, i], start=True, stop=True
                 )
                 gt[(q, t)] = g
 
@@ -178,25 +175,21 @@ def tile_model_kernel(tc, x1, dropout_mask, out):
         def tr(q, t):
             h, a = divmod(t, 2)
             if a == 0:
-                xt[(q, h)] = tps.tile([P, 2, 2, P], F32, name="xt")
+                xt[(q, h)] = tps.tile([P, 2, 2, P], F32, tag="xt", name="xt")
             words = dd[(q, t)][:].bitcast(F32)
             for u in range(2):
                 nc.tensor.transpose(xt[(q, h)][:, a, u, :], words[:, u::2], ident32[:])
 
-        def cpy(q, h, eng):
+        def cpy(q, h):
             if q not in grp:
                 grp[q] = gpool.tile([P, MT, P, MT], BF16, name="grp", align_bytes=64)
-            dst = (
-                grp[q][:, 2 * h : 2 * h + 2]
+            nc.scalar.copy(
+                out=grp[q][:, 2 * h : 2 * h + 2]
                 .rearrange("p a m c -> p (a m c)")
                 .bitcast(F32)
-                .rearrange("p (a m u) -> p a m u", a=2, u=2)
+                .rearrange("p (a m u) -> p a m u", a=2, u=2),
+                in_=xt[(q, h)][:].rearrange("p a u m -> p a m u"),
             )
-            src = xt[(q, h)][:].rearrange("p a u m -> p a m u")
-            if eng == "v":
-                nc.vector.tensor_copy(out=dst, in_=src)
-            else:
-                nc.scalar.copy(out=dst, in_=src)
 
         def quant_x(j):
             nc.vector.quantize_mx(
@@ -205,40 +198,48 @@ def tile_model_kernel(tc, x1, dropout_mask, out):
                 in_=xg[:, j].rearrange("p k c -> p (k c)"),
             )
 
-        def quant(q):
-            codes = qpool.tile([P, ROWS], U32, name="codes", align_bytes=64)
-            scl = qpool.tile([P, ROWS], U8, name="scl", align_bytes=64)
+        def quant(q, a, b):
+            if q not in cod:
+                cod[q] = (
+                    qpool.tile([P, ROWS], U32, name="codes", align_bytes=64),
+                    qpool.tile([P, ROWS], U8, name="scl", align_bytes=64),
+                )
+            codes, scl = cod[q]
             nc.vector.quantize_mx(
-                out=codes[:].bitcast(FP8X4),
-                scales=scl[:],
-                in_=grp[q][:].rearrange("p a m c -> p (a m c)"),
+                out=codes[:, a * P : b * P].bitcast(FP8X4),
+                scales=scl[:, a * P : b * P],
+                in_=grp[q][:, a:b].rearrange("p a m c -> p (a m c)"),
             )
-            cod[q] = (codes, scl)
 
-        def mx(q, spare):
+        def mx(q, a, b, spare=False):
             i, j = pairs[q]
             if spare:
-                ot[q] = gps.tile([P, MT, D], F32, tag="g", name="og")
+                o = gps.tile([P, MT, D], F32, tag="g", name="og")
             else:
-                ot[q] = ops.tile([P, MT, D], F32, name="oa")
+                o = ops.tile([P, MT, D], F32, tag="oa", name="oa")
+            ot[(q, a)] = o
             codes, scl = cod[q]
-            for a in range(MT):
+            for c in range(a, b):
                 nc.tensor.matmul_mx(
-                    out=ot[q][:, a, :],
-                    lhsT=codes[:, a * P : (a + 1) * P].bitcast(FP8X4),
-                    lhsT_scale=scl[:, a * P : (a + 1) * P],
+                    out=o[:, c, :],
+                    lhsT=codes[:, c * P : (c + 1) * P].bitcast(FP8X4),
+                    lhsT_scale=scl[:, c * P : (c + 1) * P],
                     rhs=xq[:, j * D : (j + 1) * D].bitcast(FP8X4),
                     rhs_scale=xs[:, j * D : (j + 1) * D],
                     start=True,
                     stop=True,
                 )
 
-        def ocopy_s(q):
+        def ocopy(q, a, b, eng):
             i, j = pairs[q]
-            osb[q] = opool.tile([P, MT, D], F32, name="ob")
-            nc.scalar.copy(out=osb[q][:], in_=ot[q][:])
+            ob = opool.tile([P, MT, D], F32, name="ob")
+            if eng == "v":
+                nc.vector.tensor_copy(out=ob[:, a:b], in_=ot[(q, a)][:, a:b])
+            else:
+                nc.scalar.copy(out=ob[:, a:b], in_=ot[(q, a)][:, a:b])
             nc.sync.dma_start(
-                out=out[i, j].rearrange("(p t) k -> p t k", t=MT), in_=osb[q][:]
+                out=out[i, j].rearrange("(p t) k -> p t k", t=MT)[:, a:b],
+                in_=ob[:, a:b],
             )
 
         nc.sync.dma_start(
@@ -252,47 +253,45 @@ def tile_model_kernel(tc, x1, dropout_mask, out):
 
         ctx.enter_context(tc.manual_schedule())
 
-        setup_pe(0, 1)
-        setup_s(0, 1)
-        setup_v(0)
+        setup_pe(0, "o")
+        setup_pe(0, "t")
+        setup_n(0)
+        setup_m0()
+        setup_pe(1, "o")
+        setup_n(1)
         for j in range(NG):
             setup_g(j)
         qk(0)
-        setup_pe(1, 1)
-        vmin(0, 0)
-        sexp(0, 0)
-        setup_s(1, 1)
-        for t in range(1, MT):
+        setup_pe(2, "o")
+        for t in range(MT):
             vmin(0, t)
             sexp(0, t)
-        setup_v(1)
+        setup_n(2)
         qk(1)
-        setup_pe(2, 2)
-        setup_s(2, 2)
-        setup_pe(4, 2)
 
-        last = npairs - 1
         for p in range(last):
             if p > 0:
                 gmul(p, 3)
             if p >= 3:
-                mx(p - 3, False)
+                mx(p - 3, 0, MT)
             if p >= 1:
-                cpy(p - 1, 0, "s")
+                cpy(p - 1, 0)
+                if p + 2 < NG:
+                    setup_pe(p + 2, "o")
+                    setup_n(p + 2)
             for t in range(MT):
                 vmin(p + 1, t)
                 sexp(p + 1, t)
             if p == 0:
                 recip(p)
-                setup_s(4, 2)
-            if p + 2 < NG:
-                setup_v(p + 2)
             if p + 2 < npairs:
                 qk(p + 2)
             if p >= 1:
-                cpy(p - 1, 1, "s")
+                cpy(p - 1, 1)
             if p >= 3:
-                ocopy_s(p - 3)
+                ocopy(p - 3, 0, MT, "s")
+            if p % NG == 2 and p // NG + 1 < NG:
+                setup_m(p // NG + 1)
             for t in range(MT):
                 if t < 3 or p == 0:
                     vmul(p, t)
@@ -301,25 +300,27 @@ def tile_model_kernel(tc, x1, dropout_mask, out):
                 quant_x(p - 2)
             recip(p + 1)
             if p >= 2:
-                quant(p - 2)
+                quant(p - 2, 0, MT)
             if p + PF < npairs:
                 load(p + PF)
 
-        mx(last - 3, False)
-        cpy(last - 1, 0, "s")
+        mx(last - 3, 0, MT)
+        cpy(last - 1, 0)
         for t in range(MT):
             vmul(last, t)
             tr(last, t)
-        cpy(last - 1, 1, "s")
-        quant(last - 2)
-        mx(last - 2, True)
-        ocopy_s(last - 3)
-        cpy(last, 0, "s")
-        quant(last - 1)
-        mx(last - 1, True)
-        cpy(last, 1, "v")
-        ocopy_s(last - 2)
-        quant(last)
-        mx(last, False)
-        ocopy_s(last - 1)
-        ocopy_s(last)
+        cpy(last - 1, 1)
+        ocopy(last - 3, 0, MT, "s")
+        cpy(last, 0)
+        cpy(last, 1)
+        quant(last - 2, 0, MT)
+        mx(last - 2, 0, MT, True)
+        quant(last - 1, 0, MT)
+        mx(last - 1, 0, MT, True)
+        ocopy(last - 2, 0, MT, "s")
+        for a in (0, 2):
+            quant(last, a, a + 2)
+            mx(last, a, a + 2)
+        ocopy(last - 1, 0, MT, "s")
+        ocopy(last, 0, 2, "s")
+        ocopy(last, 2, 4, "v")

@@ -24,7 +24,9 @@ PF = 8
 
 def tile_model_kernel(tc, x1, dropout_mask, out):
     nc = tc.nc
-    pairs = [(i, j) for j in range(NG) for i in range(NG)]
+    pairs = []
+    for g in range(NG):
+        pairs += [(g, j) for j in range(g)] + [(i, g) for i in range(g + 1)]
     npairs = len(pairs)
     last = npairs - 1
     with ExitStack() as ctx:
@@ -88,20 +90,17 @@ def tile_model_kernel(tc, x1, dropout_mask, out):
             stp[(g, pool)] = st
 
         def setup_n(g):
-            nc.scalar.copy(
+            nc.scalar.mul(
                 out=xtn[:, g].rearrange("k (p t) -> k p t", t=MT),
                 in_=stp[(g, "o")][:].rearrange("k t p -> k p t"),
+                mul=-1.0,
             )
 
         def setup_m0():
-            nc.vector.tensor_scalar_mul(out=xtm[:, 0], in0=stp[(0, "t")][:], scalar1=-1.0)
+            nc.vector.tensor_copy(out=xtm[:, 0], in_=stp[(0, "t")][:])
 
         def setup_m(g):
-            nc.scalar.mul(
-                out=xtm[:, g],
-                in_=xtn[:, g].rearrange("k (p t) -> k t p", t=MT),
-                mul=-1.0,
-            )
+            nc.scalar.copy(out=xtm[:, g], in_=stp[(g, "o")][:])
 
         def setup_g(j):
             nc.gpsimd.tensor_scalar(
@@ -259,15 +258,16 @@ def tile_model_kernel(tc, x1, dropout_mask, out):
         setup_m0()
         setup_pe(1, "o")
         setup_n(1)
+        setup_m(1)
         for j in range(NG):
             setup_g(j)
         qk(0)
-        setup_pe(2, "o")
         for t in range(MT):
             vmin(0, t)
             sexp(0, t)
-        setup_n(2)
         qk(1)
+        new_at = {g * g - 4: g for g in range(2, NG)}
+        xq_at = {g * g + 2: g for g in range(NG)}
 
         for p in range(last):
             if p > 0:
@@ -276,9 +276,6 @@ def tile_model_kernel(tc, x1, dropout_mask, out):
                 mx(p - 3, 0, MT)
             if p >= 1:
                 cpy(p - 1, 0)
-                if p + 2 < NG:
-                    setup_pe(p + 2, "o")
-                    setup_n(p + 2)
             for t in range(MT):
                 vmin(p + 1, t)
                 sexp(p + 1, t)
@@ -288,16 +285,18 @@ def tile_model_kernel(tc, x1, dropout_mask, out):
                 qk(p + 2)
             if p >= 1:
                 cpy(p - 1, 1)
+            if p in new_at:
+                setup_pe(new_at[p], "o")
+                setup_n(new_at[p])
+                setup_m(new_at[p])
             if p >= 3:
                 ocopy(p - 3, 0, MT, "s")
-            if p % NG == 2 and p // NG + 1 < NG:
-                setup_m(p // NG + 1)
             for t in range(MT):
                 if t < 3 or p == 0:
                     vmul(p, t)
                 tr(p, t)
-            if 0 <= p - 2 < NG:
-                quant_x(p - 2)
+            if p in xq_at:
+                quant_x(xq_at[p])
             recip(p + 1)
             if p >= 2:
                 quant(p - 2, 0, MT)

@@ -20,6 +20,8 @@ MT = 4
 FLOPS = 2 * 2 * NG * NG * ROWS * ROWS * D
 
 PF = 8
+V2 = 448
+G3 = 384
 
 
 def tile_model_kernel(tc, x1, dropout_mask, out):
@@ -32,8 +34,8 @@ def tile_model_kernel(tc, x1, dropout_mask, out):
     with ExitStack() as ctx:
         const = ctx.enter_context(tc.tile_pool(name="const", bufs=1))
         mpool = ctx.enter_context(tc.tile_pool(name="mask", bufs=PF))
-        epool = ctx.enter_context(tc.tile_pool(name="expo", bufs=12))
-        dpool = ctx.enter_context(tc.tile_pool(name="drop", bufs=6))
+        epool = ctx.enter_context(tc.tile_pool(name="expo", bufs=4))
+        dpool = ctx.enter_context(tc.tile_pool(name="drop", bufs=3))
         gpool = ctx.enter_context(tc.tile_pool(name="grouped", bufs=4))
         qpool = ctx.enter_context(tc.tile_pool(name="quant", bufs=4))
         opool = ctx.enter_context(tc.tile_pool(name="outs", bufs=4))
@@ -130,52 +132,62 @@ def tile_model_kernel(tc, x1, dropout_mask, out):
             )
 
         def sexp(q, t):
-            e = epool.tile([P, ROWS], F32, name="e")
+            if t == 0:
+                et[q] = epool.tile([P, MT, ROWS], F32, name="e")
             nc.scalar.activation(
-                out=e[:],
+                out=et[q][:, t],
                 in_=gt[(q, t)][:],
                 func=ACT.Exp,
                 bias=nmax[q][:, t : t + 1],
                 scale=-1.0,
                 accum_out=ssum[q][:, t : t + 1],
             )
-            et[(q, t)] = e
 
         def recip(q):
             rs[q] = spool.tile([P, MT], F32, name="rs")
             nc.vector.reciprocal(out=rs[q][:], in_=ssum[q][:])
 
-        def vmul(q, t):
-            d = dpool.tile([P, ROWS], BF16, name="d")
+        def vmul(q, t, w=ROWS):
+            if q not in dd:
+                dd[q] = dpool.tile([P, MT, ROWS], BF16, name="d")
             nc.vector.scalar_tensor_tensor(
-                out=d[:],
-                in0=et[(q, t)][:],
+                out=dd[q][:, t, 0:w],
+                in0=et[q][:, t, 0:w],
                 scalar=rs[q][:, t : t + 1],
-                in1=mk[q][:, t, :],
+                in1=mk[q][:, t, 0:w],
                 op0=ALU.mult,
                 op1=ALU.mult,
             )
-            dd[(q, t)] = d
 
-        def gmul(q, t):
-            d = dpool.tile([P, ROWS], BF16, name="d")
-            e = et[(q, t)]
+        def gmul(q):
+            dd[q] = dpool.tile([P, MT, ROWS], BF16, name="d")
+            cols = slice(2 * ROWS + V2, 4 * ROWS)
+            e = et[q][:].rearrange("p t n -> p (t n)")[:, cols]
+            m = mk[q][:].rearrange("p t n -> p (t n)")[:, cols]
+            nc.gpsimd.tensor_tensor(out=e, in0=e, in1=m, op=ALU.mult)
             nc.gpsimd.tensor_scalar(
-                out=e[:],
-                in0=e[:],
-                scalar1=rs[q][:, t : t + 1],
+                out=dd[q][:, 3, 0:G3],
+                in0=et[q][:, 3, 0:G3],
+                scalar1=rs[q][:, 3:4],
                 scalar2=0.0,
                 op0=ALU.mult,
                 op1=ALU.add,
             )
-            nc.gpsimd.tensor_tensor(out=d[:], in0=e[:], in1=mk[q][:, t, :], op=ALU.mult)
-            dd[(q, t)] = d
+
+        def sscale(q):
+            for t, n0 in ((2, V2), (3, G3)):
+                nc.scalar.activation(
+                    out=dd[q][:, t, n0:],
+                    in_=et[q][:, t, n0:],
+                    func=ACT.Copy,
+                    scale=rs[q][:, t : t + 1],
+                )
 
         def tr(q, t):
             h, a = divmod(t, 2)
             if a == 0:
                 xt[(q, h)] = tps.tile([P, 2, 2, P], F32, tag="xt", name="xt")
-            words = dd[(q, t)][:].bitcast(F32)
+            words = dd[q][:, t].bitcast(F32)
             for u in range(2):
                 nc.tensor.transpose(xt[(q, h)][:, a, u, :], words[:, u::2], ident32[:])
 
@@ -271,13 +283,15 @@ def tile_model_kernel(tc, x1, dropout_mask, out):
 
         for p in range(last):
             if p > 0:
-                gmul(p, 3)
+                gmul(p)
             if p >= 3:
                 mx(p - 3, 0, MT)
             if p >= 1:
                 cpy(p - 1, 0)
             for t in range(MT):
                 vmin(p + 1, t)
+                if t == 3 and p > 0:
+                    sscale(p)
                 sexp(p + 1, t)
             if p == 0:
                 recip(p)
@@ -292,8 +306,10 @@ def tile_model_kernel(tc, x1, dropout_mask, out):
             if p >= 3:
                 ocopy(p - 3, 0, MT, "s")
             for t in range(MT):
-                if t < 3 or p == 0:
+                if t < 2 or p == 0:
                     vmul(p, t)
+                elif t == 2:
+                    vmul(p, t, V2)
                 tr(p, t)
             if p in xq_at:
                 quant_x(xq_at[p])

@@ -20,8 +20,8 @@ MT = 4
 FLOPS = 2 * 2 * NG * NG * ROWS * ROWS * D
 
 PF = 8
-V2 = 448
-G3 = 384
+V2 = 416
+G3 = 352
 
 
 def tile_model_kernel(tc, x1, dropout_mask, out):
@@ -290,9 +290,9 @@ def tile_model_kernel(tc, x1, dropout_mask, out):
                 cpy(p - 1, 0)
             for t in range(MT):
                 vmin(p + 1, t)
-                if t == 3 and p > 0:
-                    sscale(p)
                 sexp(p + 1, t)
+            if p > 0:
+                sscale(p)
             if p == 0:
                 recip(p)
             if p + 2 < npairs:

@@ -165,6 +165,8 @@ def tile_model_kernel(tc, x1, dropout_mask, out):
             e = et[q][:].rearrange("p t n -> p (t n)")[:, cols]
             m = mk[q][:].rearrange("p t n -> p (t n)")[:, cols]
             nc.gpsimd.tensor_tensor(out=e, in0=e, in1=m, op=ALU.mult)
+
+        def gscale(q):
             nc.gpsimd.tensor_scalar(
                 out=dd[q][:, 3, 0:G3],
                 in0=et[q][:, 3, 0:G3],
@@ -278,7 +280,7 @@ def tile_model_kernel(tc, x1, dropout_mask, out):
             vmin(0, t)
             sexp(0, t)
         qk(1)
-        new_at = {g * g - 4: g for g in range(2, NG)}
+        new_at = {g * g - 3: g for g in range(2, NG)}
         xq_at = {g * g + 2: g for g in range(NG)}
 
         for p in range(last):
@@ -291,10 +293,12 @@ def tile_model_kernel(tc, x1, dropout_mask, out):
             for t in range(MT):
                 vmin(p + 1, t)
                 sexp(p + 1, t)
+                if t == 1:
+                    recip(p)
+                    if p > 0:
+                        gscale(p)
             if p > 0:
                 sscale(p)
-            if p == 0:
-                recip(p)
             if p + 2 < npairs:
                 qk(p + 2)
             if p >= 1:
@@ -313,12 +317,12 @@ def tile_model_kernel(tc, x1, dropout_mask, out):
                 tr(p, t)
             if p in xq_at:
                 quant_x(xq_at[p])
-            recip(p + 1)
             if p >= 2:
                 quant(p - 2, 0, MT)
             if p + PF < npairs:
                 load(p + PF)
 
+        recip(last)
         mx(last - 3, 0, MT)
         cpy(last - 1, 0)
         for t in range(MT):

from contextlib import ExitStack

import concourse.mybir as mybir
from concourse.masks import make_identity

F32 = mybir.dt.float32
BF16 = mybir.dt.bfloat16
U32 = mybir.dt.uint32
U8 = mybir.dt.uint8
FP8X4 = mybir.dt.float8_e4m3fn_x4
ACT = mybir.ActivationFunctionType
ALU = mybir.AluOpType
AX = mybir.AxisListType

NG = 6
ROWS = 512
D = 128
P = 128
MT = 4
FLOPS = 2 * 2 * NG * NG * ROWS * ROWS * D

PF = 8
V2 = 416
G3 = 352


def tile_model_kernel(tc, x1, dropout_mask, out):
    nc = tc.nc
    pairs = []
    for g in range(NG):
        pairs += [(g, j) for j in range(g)] + [(i, g) for i in range(g + 1)]
    npairs = len(pairs)
    last = npairs - 1
    with ExitStack() as ctx:
        const = ctx.enter_context(tc.tile_pool(name="const", bufs=1))
        mpool = ctx.enter_context(tc.tile_pool(name="mask", bufs=PF))
        epool = ctx.enter_context(tc.tile_pool(name="expo", bufs=4))
        dpool = ctx.enter_context(tc.tile_pool(name="drop", bufs=3))
        gpool = ctx.enter_context(tc.tile_pool(name="grouped", bufs=4))
        qpool = ctx.enter_context(tc.tile_pool(name="quant", bufs=4))
        opool = ctx.enter_context(tc.tile_pool(name="outs", bufs=4))
        spool = ctx.enter_context(tc.tile_pool(name="stats", bufs=5))
        gps = ctx.enter_context(tc.psum_pool(name="gps", bufs=4))
        tps = ctx.enter_context(tc.psum_pool(name="tps", bufs=2))
        ops = ctx.enter_context(tc.psum_pool(name="ops", bufs=2))

        warm = const.tile([P, 1], F32, name="warm")
        warm2 = const.tile([P, 1], F32, name="warm2")
        nc.vector.memset(warm[:], 0.0)
        nc.scalar.activation(out=warm2[:], in_=warm[:], func=ACT.Exp)

        ident = const.tile([P, P], BF16, name="ident")
        make_identity(nc, ident[:])
        ident32 = const.tile([P, P], F32, name="ident32")
        make_identity(nc, ident32[:])

        xc = const.tile([P, NG, MT, D], BF16, name="xc")
        xtm = const.tile([P, NG, MT, P], BF16, name="xtm")
        xtn = const.tile([P, NG, ROWS], BF16, name="xtn")
        xg = const.tile([P, NG, D, MT], BF16, name="xg", align_bytes=64)
        xq = const.tile([P, NG * D], U32, name="xq", align_bytes=64)
        xs = const.tile([P, NG * D], U8, name="xs", align_bytes=64)

        mk = {}
        nmax = {}
        ssum = {}
        rs = {}
        gt = {}
        et = {}
        dd = {}
        xt = {}
        grp = {}
        cod = {}
        ot = {}
        stp = {}

        def load(q):
            i, j = pairs[q]
            m = mpool.tile([P, MT, ROWS], BF16, name="mk")
            nc.sync.dma_start(
                out=m[:], in_=dropout_mask[i, j].rearrange("(p t) n -> p t n", t=MT)
            )
            mk[q] = m

        def setup_pe(g, pool):
            if pool == "t":
                st = tps.tile([P, MT, P], BF16, tag="xt", name="stt")
            else:
                st = ops.tile([P, MT, P], BF16, tag="oa", name="sto")
            for c in range(MT):
                nc.tensor.transpose(st[:, c, :], xc[:, g, c, :], ident[:])
            stp[(g, pool)] = st

        def setup_n(g):
            nc.scalar.mul(
                out=xtn[:, g].rearrange("k (p t) -> k p t", t=MT),
                in_=stp[(g, "o")][:].rearrange("k t p -> k p t"),
                mul=-1.0,
            )

        def setup_m0():
            nc.vector.tensor_copy(out=xtm[:, 0], in_=stp[(0, "t")][:])

        def setup_m(g):
            nc.scalar.copy(out=xtm[:, g], in_=stp[(g, "o")][:])

        def setup_g(j):
            nc.gpsimd.tensor_scalar(
                out=xg[:, j],
                in0=xc[:, j].rearrange("p c k -> p k c"),
                scalar1=1.0,
                scalar2=0.0,
                op0=ALU.mult,
                op1=ALU.add,
            )

        def qk(q):
            i, j = pairs[q]
            for t in range(MT):
                g = gps.tile([P, ROWS], F32, tag="g", name="g")
                nc.tensor.matmul(
                    out=g[:], lhsT=xtm[:, j, t, :], rhs=xtn[:, i], start=True, stop=True
                )
                gt[(q, t)] = g

        def vmin(q, t):
            if t == 0:
                nmax[q] = spool.tile([P, MT], F32, name="nmax")
                ssum[q] = spool.tile([P, MT], F32, name="ssum")
            nc.vector.tensor_reduce(
                out=nmax[q][:, t : t + 1], in_=gt[(q, t)][:], axis=AX.X, op=ALU.min
            )

        def sexp(q, t):
            if t == 0:
                et[q] = epool.tile([P, MT, ROWS], F32, name="e")
            nc.scalar.activation(
                out=et[q][:, t],
                in_=gt[(q, t)][:],
                func=ACT.Exp,
                bias=nmax[q][:, t : t + 1],
                scale=-1.0,
                accum_out=ssum[q][:, t : t + 1],
            )

        def recip(q):
            rs[q] = spool.tile([P, MT], F32, name="rs")
            nc.vector.reciprocal(out=rs[q][:], in_=ssum[q][:])

        def vmul(q, t, w=ROWS):
            if q not in dd:
                dd[q] = dpool.tile([P, MT, ROWS], BF16, name="d")
            nc.vector.scalar_tensor_tensor(
                out=dd[q][:, t, 0:w],
                in0=et[q][:, t, 0:w],
                scalar=rs[q][:, t : t + 1],
                in1=mk[q][:, t, 0:w],
                op0=ALU.mult,
                op1=ALU.mult,
            )

        def gmul(q):
            dd[q] = dpool.tile([P, MT, ROWS], BF16, name="d")
            cols = slice(2 * ROWS + V2, 4 * ROWS)
            e = et[q][:].rearrange("p t n -> p (t n)")[:, cols]
            m = mk[q][:].rearrange("p t n -> p (t n)")[:, cols]
            nc.gpsimd.tensor_tensor(out=e, in0=e, in1=m, op=ALU.mult)

        def gscale(q):
            nc.gpsimd.tensor_scalar(
                out=dd[q][:, 3, 0:G3],
                in0=et[q][:, 3, 0:G3],
                scalar1=rs[q][:, 3:4],
                scalar2=0.0,
                op0=ALU.mult,
                op1=ALU.add,
            )

        def sscale(q):
            for t, n0 in ((2, V2), (3, G3)):
                nc.scalar.activation(
                    out=dd[q][:, t, n0:],
                    in_=et[q][:, t, n0:],
                    func=ACT.Copy,
                    scale=rs[q][:, t : t + 1],
                )

        def tr(q, t):
            h, a = divmod(t, 2)
            if a == 0:
                xt[(q, h)] = tps.tile([P, 2, 2, P], F32, tag="xt", name="xt")
            words = dd[q][:, t].bitcast(F32)
            for u in range(2):
                nc.tensor.transpose(xt[(q, h)][:, a, u, :], words[:, u::2], ident32[:])

        def cpy(q, h):
            if q not in grp:
                grp[q] = gpool.tile([P, MT, P, MT], BF16, name="grp", align_bytes=64)
            nc.scalar.copy(
                out=grp[q][:, 2 * h : 2 * h + 2]
                .rearrange("p a m c -> p (a m c)")
                .bitcast(F32)
                .rearrange("p (a m u) -> p a m u", a=2, u=2),
                in_=xt[(q, h)][:].rearrange("p a u m -> p a m u"),
            )

        def quant_x(j):
            nc.vector.quantize_mx(
                out=xq[:, j * D : (j + 1) * D].bitcast(FP8X4),
                scales=xs[:, j * D : (j + 1) * D],
                in_=xg[:, j].rearrange("p k c -> p (k c)"),
            )

        def quant(q, a, b):
            if q not in cod:
                cod[q] = (
                    qpool.tile([P, ROWS], U32, name="codes", align_bytes=64),
                    qpool.tile([P, ROWS], U8, name="scl", align_bytes=64),
                )
            codes, scl = cod[q]
            nc.vector.quantize_mx(
                out=codes[:, a * P : b * P].bitcast(FP8X4),
                scales=scl[:, a * P : b * P],
                in_=grp[q][:, a:b].rearrange("p a m c -> p (a m c)"),
            )

        def mx(q, a, b, spare=False):
            i, j = pairs[q]
            if spare:
                o = gps.tile([P, MT, D], F32, tag="g", name="og")
            else:
                o = ops.tile([P, MT, D], F32, tag="oa", name="oa")
            ot[(q, a)] = o
            codes, scl = cod[q]
            for c in range(a, b):
                nc.tensor.matmul_mx(
                    out=o[:, c, :],
                    lhsT=codes[:, c * P : (c + 1) * P].bitcast(FP8X4),
                    lhsT_scale=scl[:, c * P : (c + 1) * P],
                    rhs=xq[:, j * D : (j + 1) * D].bitcast(FP8X4),
                    rhs_scale=xs[:, j * D : (j + 1) * D],
                    start=True,
                    stop=True,
                )

        def ocopy(q, a, b, eng):
            i, j = pairs[q]
            ob = opool.tile([P, MT, D], F32, name="ob")
            if eng == "v":
                nc.vector.tensor_copy(out=ob[:, a:b], in_=ot[(q, a)][:, a:b])
            else:
                nc.scalar.copy(out=ob[:, a:b], in_=ot[(q, a)][:, a:b])
            nc.sync.dma_start(
                out=out[i, j].rearrange("(p t) k -> p t k", t=MT)[:, a:b],
                in_=ob[:, a:b],
            )

        nc.sync.dma_start(
            out=xc[:, 0], in_=x1[0, 0].rearrange("(p c) k -> p c k", c=MT)
        )
        nc.sync.dma_start(
            out=xc[:, 1:], in_=x1[0, 1:].rearrange("j (p c) k -> p j c k", c=MT)
        )
        for q in range(PF):
            load(q)

        ctx.enter_context(tc.manual_schedule())

        setup_pe(0, "o")
        setup_pe(0, "t")
        setup_n(0)
        setup_m0()
        setup_pe(1, "o")
        setup_n(1)
        setup_m(1)
        for j in range(NG):
            setup_g(j)
        qk(0)
        for t in range(MT):
            vmin(0, t)
            sexp(0, t)
        qk(1)
        new_at = {g * g - 3: g for g in range(2, NG)}
        xq_at = {g * g + 2: g for g in range(NG)}

        for p in range(last):
            if p > 0:
                gmul(p)
            if p >= 3:
                mx(p - 3, 0, MT)
            if p >= 1:
                cpy(p - 1, 0)
            for t in range(MT):
                vmin(p + 1, t)
                sexp(p + 1, t)
                if t == 1:
                    recip(p)
                    if p > 0:
                        gscale(p)
            if p > 0:
                sscale(p)
            if p + 2 < npairs:
                qk(p + 2)
            if p >= 1:
                cpy(p - 1, 1)
            if p in new_at:
                setup_pe(new_at[p], "o")
                setup_n(new_at[p])
                setup_m(new_at[p])
            if p >= 3:
                ocopy(p - 3, 0, MT, "s")
            for t in range(MT):
                if t < 2 or p == 0:
                    vmul(p, t)
                elif t == 2:
                    vmul(p, t, V2)
                tr(p, t)
            if p in xq_at:
                quant_x(xq_at[p])
            if p >= 2:
                quant(p - 2, 0, MT)
            if p + PF < npairs:
                load(p + PF)

        recip(last)
        mx(last - 3, 0, MT)
        cpy(last - 1, 0)
        for t in range(MT):
            vmul(last, t)
            tr(last, t)
        cpy(last - 1, 1)
        ocopy(last - 3, 0, MT, "s")
        cpy(last, 0)
        cpy(last, 1)
        quant(last - 2, 0, MT)
        mx(last - 2, 0, MT, True)
        quant(last - 1, 0, MT)
        mx(last - 1, 0, MT, True)
        ocopy(last - 2, 0, MT, "s")
        for a in (0, 2):
            quant(last, a, a + 2)
            mx(last, a, a + 2)
        ocopy(last - 1, 0, MT, "s")
        ocopy(last, 0, 2, "s")
        ocopy(last, 2, 4, "v")
